import numpy as np
import ml_dtypes


def mxq(x, axis, fmt="e4m3"):
    dtype, down = {"e4m3": (ml_dtypes.float8_e4m3fn, 7), "e5m2": (ml_dtypes.float8_e5m2, 14)}[fmt]
    v = np.moveaxis(np.asarray(x, np.float32).astype(ml_dtypes.bfloat16).astype(np.float64), axis, -1)
    blocks = v.reshape(v.shape[:-1] + (-1, 32))
    amax = np.abs(blocks).max(-1, keepdims=True)
    byte = np.maximum(np.where(amax > 0, np.frexp(amax)[1] - 1 + 127, 0) - down, 1)
    scale = np.exp2(byte - 127.0)
    codes = (blocks / scale).astype(np.float32).astype(dtype).astype(np.float64)
    return np.moveaxis((codes * scale).reshape(v.shape), -1, axis)


WIDE = False


def mx_kscale(k):
    if not WIDE:
        return np.ones(k)
    levels = np.array([10, -10, 5, -5, 0])
    a = np.random.permutation(np.resize(levels, k // 512 * 4)).reshape(k // 512, 4)
    idx = np.arange(k)
    return np.exp2(a[idx // 512, idx % 128 // 32])


BF16 = ml_dtypes.bfloat16


def bf(x):
    return np.asarray(x, np.float32).astype(BF16)


def f64(x):
    return np.asarray(x).astype(np.float64)


B, S, D, BD, K = 4, 128, 512, 512, 128
TS = 3.0


def sigmoid(v):
    return 1.0 / (1.0 + np.exp(-v))


def setup_inputs():
    s = mx_kscale(D)
    return {
        "token_embeddings": bf(np.random.standard_normal((B, S, D)) * TS * s),
        "splat_influences": bf(np.random.uniform(size=(B, S, K))),
        "decoded": bf(np.random.standard_normal((B, K, D)) * 0.35),
        "gate_W": bf(np.random.standard_normal((D, D)) / (TS * np.sqrt(D)) / s[:, None]),
        "gate_b": bf(np.random.standard_normal(D) * 0.5),
    }


def reference(token_embeddings, splat_influences, decoded, gate_W, gate_b):
    flow = f64(splat_influences) @ f64(decoded)
    gate = sigmoid((mxq(f64(token_embeddings), 2, "e4m3") @ mxq(f64(gate_W), 0, "e4m3")) + f64(gate_b))
    return flow * gate

@@ -1,0 +1,129 @@
+from contextlib import ExitStack
+
+import concourse.mybir as mybir
+from concourse.masks import make_identity
+
+F32 = mybir.dt.float32
+BF16 = mybir.dt.bfloat16
+U32 = mybir.dt.uint32
+U8 = mybir.dt.uint8
+FP8X4 = mybir.dt.float8_e4m3fn_x4
+ADD = mybir.AluOpType.add
+MULT = mybir.AluOpType.mult
+SIGMOID = mybir.ActivationFunctionType.Sigmoid
+
+P = 128
+B = 4
+D = 512
+PACK = 4
+HALVES = 2
+PAIR = 2
+
+FLOPS = 2 * B * P * D * D + 2 * B * P * P * D
+
+
+def tile_splatinformationflow_pb_s_kernel(
+    tc, token_embeddings, splat_influences, decoded, gate_W, gate_b, out
+):
+    nc = tc.nc
+    with ExitStack() as ctx:
+        keep = ctx.enter_context(tc.tile_pool(name="keep", bufs=1))
+        work = ctx.enter_context(tc.tile_pool(name="work", bufs=B))
+        psum = ctx.enter_context(tc.psum_pool(name="psum", bufs=1))
+
+        bias_row = keep.tile([P, D], BF16)
+        nc.vector.memset(bias_row[:], 0.0)
+        nc.scalar.dma_start(out=bias_row[0:1, :], in_=gate_b.rearrange("(o n) -> o n", o=1))
+        w_rows = keep.tile([P, PACK, D], BF16)
+        nc.sync.dma_start(
+            out=w_rows[:].rearrange("q (u e) n -> q u e n", u=HALVES),
+            in_=gate_W.rearrange("(u q e) n -> q u e n", u=HALVES, e=2),
+        )
+        x_rows = keep.tile([P, B * D], BF16)
+        for h in range(B // PAIR):
+            nc.sync.dma_start(
+                out=x_rows[:, h * PAIR * D : (h + 1) * PAIR * D].rearrange("s (b d) -> s b d", b=PAIR),
+                in_=token_embeddings[h * PAIR : (h + 1) * PAIR].rearrange("b s d -> s b d"),
+            )
+        infl_rows = keep.tile([P, B, P], BF16)
+        nc.sync.dma_start(out=infl_rows[:], in_=splat_influences.rearrange("b s k -> s b k"))
+        dec_rows = keep.tile([P, B, D], BF16)
+        nc.sync.dma_start(out=dec_rows[:], in_=decoded.rearrange("b k d -> k b d"))
+
+        warm = keep.tile([P, 1], F32)
+        nc.vector.memset(warm[:], 0.0)
+        nc.scalar.activation(out=warm[:], in_=warm[:], func=SIGMOID)
+        ident_f32 = keep.tile([P, P], F32)
+        make_identity(nc, ident_f32[:])
+        ident_bf16 = keep.tile([P, P], BF16)
+        make_identity(nc, ident_bf16[:])
+
+        ones = keep.tile([P, P], BF16)
+        nc.vector.memset(ones[:], 1.0)
+        bias_ps = psum.tile([P, D], F32, tag="early0")
+        nc.tensor.matmul(out=bias_ps[:], lhsT=ones[:], rhs=bias_row[:], start=True, stop=True)
+        bias_all = keep.tile([P, D], F32)
+        nc.scalar.copy(out=bias_all[:], in_=bias_ps[:])
+
+        w_grouped = keep.tile([P, D, PACK], BF16, align_bytes=64)
+        nc.vector.tensor_copy(
+            out=w_grouped[:].rearrange("p (c i) t -> p c t i", i=4),
+            in_=w_rows[:].rearrange("p t (c i) -> p c t i", i=4),
+        )
+        w_codes = keep.tile([P, D], U32, align_bytes=64)
+        w_scales = keep.tile([P, D], U8, align_bytes=64)
+        nc.vector.quantize_mx(
+            out=w_codes[:].bitcast(FP8X4),
+            scales=w_scales[:],
+            in_=w_grouped[:].rearrange("p n t -> p (n t)"),
+        )
+
+        x_words = x_rows[:].bitcast(F32)
+        x_grouped = keep.tile([P, B * P * PACK], BF16, align_bytes=64)
+        x_grouped_words = x_grouped[:].bitcast(F32)
+        x_codes = keep.tile([P, B * P], U32, align_bytes=64)
+        x_scales = keep.tile([P, B * P], U8, align_bytes=64)
+        for h in range(B // PAIR):
+            xt_ps = psum.tile([P, PAIR, HALVES, P], F32, tag="early%d" % (1 + h))
+            for i in range(PAIR):
+                for u in range(HALVES):
+                    first = ((h * PAIR + i) * HALVES + u) * P
+                    nc.tensor.transpose(xt_ps[:, i, u, :], x_words[:, first : first + P], ident_f32[:])
+            nc.scalar.copy(
+                out=x_grouped_words[:, h * PAIR * P * HALVES : (h + 1) * PAIR * P * HALVES].rearrange(
+                    "p (i s u) -> p i s u", i=PAIR, u=HALVES
+                ),
+                in_=xt_ps[:].rearrange("p i u s -> p i s u"),
+            )
+            nc.vector.quantize_mx(
+                out=x_codes[:, h * PAIR * P : (h + 1) * PAIR * P].bitcast(FP8X4),
+                scales=x_scales[:, h * PAIR * P : (h + 1) * PAIR * P],
+                in_=x_grouped[:, h * PAIR * P * PACK : (h + 1) * PAIR * P * PACK],
+            )
+
+        inflT_ps = psum.tile([P, B, P], BF16, tag="early3")
+        for b in range(B):
+            nc.tensor.transpose(inflT_ps[:, b, :], infl_rows[:, b, :], ident_bf16[:])
+        inflT = keep.tile([P, B, P], BF16)
+        nc.scalar.copy(out=inflT[:], in_=inflT_ps[:])
+
+        for b in range(B):
+            gate_ps = psum.tile([P, D], F32, tag="gate%d" % b)
+            nc.tensor.matmul_mx(
+                out=gate_ps[:],
+                lhsT=x_codes[:, b * P : (b + 1) * P].bitcast(FP8X4),
+                lhsT_scale=x_scales[:, b * P : (b + 1) * P],
+                rhs=w_codes[:].bitcast(FP8X4),
+                rhs_scale=w_scales[:],
+                start=True,
+                stop=True,
+            )
+            flow_ps = psum.tile([P, D], F32, tag="early%d" % b)
+            nc.tensor.matmul(out=flow_ps[:], lhsT=inflT[:, b, :], rhs=dec_rows[:, b, :], start=True, stop=True)
+            logits = work.tile([P, D], F32)
+            nc.vector.tensor_tensor(out=logits[:], in0=gate_ps[:], in1=bias_all[:], op=ADD)
+            gate = work.tile([P, D], F32)
+            nc.scalar.activation(out=gate[:], in_=logits[:], func=SIGMOID)
+            result = work.tile([P, D], F32)
+            nc.vector.tensor_tensor(out=result[:], in0=flow_ps[:], in1=gate[:], op=MULT)
+            nc.sync.dma_start(out=out[b], in_=result[:])

@@ -7,6 +7,7 @@ F32 = mybir.dt.float32
 BF16 = mybir.dt.bfloat16
 U32 = mybir.dt.uint32
 U8 = mybir.dt.uint8
+I32 = mybir.dt.int32
 FP8X4 = mybir.dt.float8_e4m3fn_x4
 ADD = mybir.AluOpType.add
 MULT = mybir.AluOpType.mult
@@ -18,6 +19,7 @@ D = 512
 PACK = 4
 HALVES = 2
 PAIR = 2
+W_PARTS = 2
 
 FLOPS = 2 * B * P * D * D + 2 * B * P * P * D
 
@@ -30,9 +32,10 @@ def tile_splatinformationflow_pb_s_kernel(
         keep = ctx.enter_context(tc.tile_pool(name="keep", bufs=1))
         work = ctx.enter_context(tc.tile_pool(name="work", bufs=B))
         psum = ctx.enter_context(tc.psum_pool(name="psum", bufs=1))
+        ctx.enter_context(tc.manual_schedule())
 
         bias_row = keep.tile([P, D], BF16)
-        nc.vector.memset(bias_row[:], 0.0)
+        nc.vector.memset(bias_row[:].bitcast(I32), 0)
         nc.scalar.dma_start(out=bias_row[0:1, :], in_=gate_b.rearrange("(o n) -> o n", o=1))
         w_rows = keep.tile([P, PACK, D], BF16)
         nc.sync.dma_start(
@@ -66,17 +69,20 @@ def tile_splatinformationflow_pb_s_kernel(
         nc.scalar.copy(out=bias_all[:], in_=bias_ps[:])
 
         w_grouped = keep.tile([P, D, PACK], BF16, align_bytes=64)
-        nc.vector.tensor_copy(
-            out=w_grouped[:].rearrange("p (c i) t -> p c t i", i=4),
-            in_=w_rows[:].rearrange("p t (c i) -> p c t i", i=4),
-        )
         w_codes = keep.tile([P, D], U32, align_bytes=64)
         w_scales = keep.tile([P, D], U8, align_bytes=64)
-        nc.vector.quantize_mx(
-            out=w_codes[:].bitcast(FP8X4),
-            scales=w_scales[:],
-            in_=w_grouped[:].rearrange("p n t -> p (n t)"),
-        )
+        w_cols = [slice(c * D // W_PARTS, (c + 1) * D // W_PARTS) for c in range(W_PARTS)]
+        for cols in w_cols:
+            nc.vector.tensor_copy(
+                out=w_grouped[:, cols, :].rearrange("p (c i) t -> p c t i", i=4),
+                in_=w_rows[:, :, cols].rearrange("p t (c i) -> p c t i", i=4),
+            )
+        for cols in w_cols:
+            nc.vector.quantize_mx(
+                out=w_codes[:, cols].bitcast(FP8X4),
+                scales=w_scales[:, cols],
+                in_=w_grouped[:, cols, :].rearrange("p n t -> p (n t)"),
+            )
 
         x_words = x_rows[:].bitcast(F32)
         x_grouped = keep.tile([P, B * P * PACK], BF16, align_bytes=64)
@@ -107,7 +113,9 @@ def tile_splatinformationflow_pb_s_kernel(
         inflT = keep.tile([P, B, P], BF16)
         nc.scalar.copy(out=inflT[:], in_=inflT_ps[:])
 
-        for b in range(B):
+        gates = []
+
+        def gate_of(b):
             gate_ps = psum.tile([P, D], F32, tag="gate%d" % b)
             nc.tensor.matmul_mx(
                 out=gate_ps[:],
@@ -118,12 +126,21 @@ def tile_splatinformationflow_pb_s_kernel(
                 start=True,
                 stop=True,
             )
-            flow_ps = psum.tile([P, D], F32, tag="early%d" % b)
-            nc.tensor.matmul(out=flow_ps[:], lhsT=inflT[:, b, :], rhs=dec_rows[:, b, :], start=True, stop=True)
             logits = work.tile([P, D], F32)
             nc.vector.tensor_tensor(out=logits[:], in0=gate_ps[:], in1=bias_all[:], op=ADD)
             gate = work.tile([P, D], F32)
             nc.scalar.activation(out=gate[:], in_=logits[:], func=SIGMOID)
+            gates.append(gate)
+
+        def gated_flow_of(b):
+            flow_ps = psum.tile([P, D], F32, tag="early%d" % b)
+            nc.tensor.matmul(out=flow_ps[:], lhsT=inflT[:, b, :], rhs=dec_rows[:, b, :], start=True, stop=True)
             result = work.tile([P, D], F32)
-            nc.vector.tensor_tensor(out=result[:], in0=flow_ps[:], in1=gate[:], op=MULT)
+            nc.vector.tensor_tensor(out=result[:], in0=flow_ps[:], in1=gates[b][:], op=MULT)
             nc.sync.dma_start(out=out[b], in_=result[:])
+
+        gate_of(0)
+        for b in range(1, B):
+            gate_of(b)
+            gated_flow_of(b - 1)
+        gated_flow_of(B - 1)

@@ -18,7 +18,8 @@ B = 4
 D = 512
 PACK = 4
 HALVES = 2
-PAIR = 2
+LAG = 2
+BANKS = 8
 W_PARTS = 2
 
 FLOPS = 2 * B * P * D * D + 2 * B * P * P * D
@@ -31,7 +32,7 @@ def tile_splatinformationflow_pb_s_kernel(
     with ExitStack() as ctx:
         keep = ctx.enter_context(tc.tile_pool(name="keep", bufs=1))
         work = ctx.enter_context(tc.tile_pool(name="work", bufs=B))
-        psum = ctx.enter_context(tc.psum_pool(name="psum", bufs=1))
+        psum = ctx.enter_context(tc.psum_pool(name="psum", bufs=BANKS))
         ctx.enter_context(tc.manual_schedule())
 
         bias_row = keep.tile([P, D], BF16)
@@ -43,11 +44,8 @@ def tile_splatinformationflow_pb_s_kernel(
             in_=gate_W.rearrange("(u q e) n -> q u e n", u=HALVES, e=2),
         )
         x_rows = keep.tile([P, B * D], BF16)
-        for h in range(B // PAIR):
-            nc.sync.dma_start(
-                out=x_rows[:, h * PAIR * D : (h + 1) * PAIR * D].rearrange("s (b d) -> s b d", b=PAIR),
-                in_=token_embeddings[h * PAIR : (h + 1) * PAIR].rearrange("b s d -> s b d"),
-            )
+        for b in range(B):
+            nc.sync.dma_start(out=x_rows[:, b * D : (b + 1) * D], in_=token_embeddings[b])
         infl_rows = keep.tile([P, B, P], BF16)
         nc.sync.dma_start(out=infl_rows[:], in_=splat_influences.rearrange("b s k -> s b k"))
         dec_rows = keep.tile([P, B, D], BF16)
@@ -63,7 +61,7 @@ def tile_splatinformationflow_pb_s_kernel(
 
         ones = keep.tile([P, P], BF16)
         nc.vector.memset(ones[:], 1.0)
-        bias_ps = psum.tile([P, D], F32, tag="early0")
+        bias_ps = psum.tile([P, D], F32, tag="bank")
         nc.tensor.matmul(out=bias_ps[:], lhsT=ones[:], rhs=bias_row[:], start=True, stop=True)
         bias_all = keep.tile([P, D], F32)
         nc.scalar.copy(out=bias_all[:], in_=bias_ps[:])
@@ -89,25 +87,22 @@ def tile_splatinformationflow_pb_s_kernel(
         x_grouped_words = x_grouped[:].bitcast(F32)
         x_codes = keep.tile([P, B * P], U32, align_bytes=64)
         x_scales = keep.tile([P, B * P], U8, align_bytes=64)
-        for h in range(B // PAIR):
-            xt_ps = psum.tile([P, PAIR, HALVES, P], F32, tag="early%d" % (1 + h))
-            for i in range(PAIR):
-                for u in range(HALVES):
-                    first = ((h * PAIR + i) * HALVES + u) * P
-                    nc.tensor.transpose(xt_ps[:, i, u, :], x_words[:, first : first + P], ident_f32[:])
+        for b in range(B):
+            xt_ps = psum.tile([P, HALVES, P], F32, tag="bank")
+            for u in range(HALVES):
+                first = (b * HALVES + u) * P
+                nc.tensor.transpose(xt_ps[:, u, :], x_words[:, first : first + P], ident_f32[:])
             nc.scalar.copy(
-                out=x_grouped_words[:, h * PAIR * P * HALVES : (h + 1) * PAIR * P * HALVES].rearrange(
-                    "p (i s u) -> p i s u", i=PAIR, u=HALVES
-                ),
-                in_=xt_ps[:].rearrange("p i u s -> p i s u"),
+                out=x_grouped_words[:, b * P * HALVES : (b + 1) * P * HALVES].rearrange("p (s u) -> p s u", u=HALVES),
+                in_=xt_ps[:].rearrange("p u s -> p s u"),
             )
             nc.vector.quantize_mx(
-                out=x_codes[:, h * PAIR * P : (h + 1) * PAIR * P].bitcast(FP8X4),
-                scales=x_scales[:, h * PAIR * P : (h + 1) * PAIR * P],
-                in_=x_grouped[:, h * PAIR * P * PACK : (h + 1) * PAIR * P * PACK],
+                out=x_codes[:, b * P : (b + 1) * P].bitcast(FP8X4),
+                scales=x_scales[:, b * P : (b + 1) * P],
+                in_=x_grouped[:, b * P * PACK : (b + 1) * P * PACK],
             )
 
-        inflT_ps = psum.tile([P, B, P], BF16, tag="early3")
+        inflT_ps = psum.tile([P, B, P], BF16, tag="bank")
         for b in range(B):
             nc.tensor.transpose(inflT_ps[:, b, :], infl_rows[:, b, :], ident_bf16[:])
         inflT = keep.tile([P, B, P], BF16)
@@ -116,7 +111,7 @@ def tile_splatinformationflow_pb_s_kernel(
         gates = []
 
         def gate_of(b):
-            gate_ps = psum.tile([P, D], F32, tag="gate%d" % b)
+            gate_ps = psum.tile([P, D], F32, tag="bank")
             nc.tensor.matmul_mx(
                 out=gate_ps[:],
                 lhsT=x_codes[:, b * P : (b + 1) * P].bitcast(FP8X4),
@@ -133,14 +128,14 @@ def tile_splatinformationflow_pb_s_kernel(
             gates.append(gate)
 
         def gated_flow_of(b):
-            flow_ps = psum.tile([P, D], F32, tag="early%d" % b)
+            flow_ps = psum.tile([P, D], F32, tag="bank")
             nc.tensor.matmul(out=flow_ps[:], lhsT=inflT[:, b, :], rhs=dec_rows[:, b, :], start=True, stop=True)
             result = work.tile([P, D], F32)
             nc.vector.tensor_tensor(out=result[:], in0=flow_ps[:], in1=gates[b][:], op=MULT)
             nc.sync.dma_start(out=out[b], in_=result[:])
 
-        gate_of(0)
-        for b in range(1, B):
-            gate_of(b)
-            gated_flow_of(b - 1)
-        gated_flow_of(B - 1)
+        for b in range(B + LAG):
+            if b < B:
+                gate_of(b)
+            if b >= LAG:
+                gated_flow_of(b - LAG)

@@ -20,6 +20,7 @@ PACK = 4
 HALVES = 2
 LAG = 2
 BANKS = 8
+ROWS = B
 W_PARTS = 2
 
 FLOPS = 2 * B * P * D * D + 2 * B * P * P * D
@@ -35,19 +36,21 @@ def tile_splatinformationflow_pb_s_kernel(
         psum = ctx.enter_context(tc.psum_pool(name="psum", bufs=BANKS))
         ctx.enter_context(tc.manual_schedule())
 
-        bias_row = keep.tile([P, D], BF16)
-        nc.vector.memset(bias_row[:].bitcast(I32), 0)
-        nc.scalar.dma_start(out=bias_row[0:1, :], in_=gate_b.rearrange("(o n) -> o n", o=1))
         w_rows = keep.tile([P, PACK, D], BF16)
         nc.sync.dma_start(
             out=w_rows[:].rearrange("q (u e) n -> q u e n", u=HALVES),
             in_=gate_W.rearrange("(u q e) n -> q u e n", u=HALVES, e=2),
         )
+        bias_row = keep.tile([P, D], BF16)
+        nc.vector.memset(bias_row[:].bitcast(I32), 0)
+        nc.sync.dma_start(out=bias_row[0:1, :], in_=gate_b.rearrange("(o n) -> o n", o=1))
         x_rows = keep.tile([P, B * D], BF16)
         for b in range(B):
             nc.sync.dma_start(out=x_rows[:, b * D : (b + 1) * D], in_=token_embeddings[b])
-        infl_rows = keep.tile([P, B, P], BF16)
-        nc.sync.dma_start(out=infl_rows[:], in_=splat_influences.rearrange("b s k -> s b k"))
+        infl_rows = keep.tile([P, ROWS, P], BF16)
+        nc.sync.dma_start(
+            out=infl_rows[:], in_=splat_influences.flatten_outer_dims().rearrange("(p r) k -> p r k", r=ROWS)
+        )
         dec_rows = keep.tile([P, B, D], BF16)
         nc.sync.dma_start(out=dec_rows[:], in_=decoded.rearrange("b k d -> k b d"))
 
@@ -102,11 +105,11 @@ def tile_splatinformationflow_pb_s_kernel(
                 in_=x_grouped[:, b * P * PACK : (b + 1) * P * PACK],
             )
 
-        inflT_ps = psum.tile([P, B, P], BF16, tag="bank")
-        for b in range(B):
-            nc.tensor.transpose(inflT_ps[:, b, :], infl_rows[:, b, :], ident_bf16[:])
-        inflT = keep.tile([P, B, P], BF16)
-        nc.scalar.copy(out=inflT[:], in_=inflT_ps[:])
+        inflT_ps = psum.tile([P, ROWS, P], BF16, tag="bank")
+        for r in range(ROWS):
+            nc.tensor.transpose(inflT_ps[:, r, :], infl_rows[:, r, :], ident_bf16[:])
+        inflT = keep.tile([P, B * P], BF16)
+        nc.scalar.copy(out=inflT[:].rearrange("k (p r) -> k p r", r=ROWS), in_=inflT_ps[:].rearrange("k r p -> k p r"))
 
         gates = []
 
@@ -129,7 +132,7 @@ def tile_splatinformationflow_pb_s_kernel(
 
         def gated_flow_of(b):
             flow_ps = psum.tile([P, D], F32, tag="bank")
-            nc.tensor.matmul(out=flow_ps[:], lhsT=inflT[:, b, :], rhs=dec_rows[:, b, :], start=True, stop=True)
+            nc.tensor.matmul(out=flow_ps[:], lhsT=inflT[:, b * P : (b + 1) * P], rhs=dec_rows[:, b, :], start=True, stop=True)
             result = work.tile([P, D], F32)
             nc.vector.tensor_tensor(out=result[:], in0=flow_ps[:], in1=gates[b][:], op=MULT)
             nc.sync.dma_start(out=out[b], in_=result[:])

@@ -21,7 +21,6 @@ HALVES = 2
 LAG = 2
 BANKS = 8
 ROWS = B
-W_PARTS = 2
 
 FLOPS = 2 * B * P * D * D + 2 * B * P * P * D
 
@@ -36,14 +35,15 @@ def tile_splatinformationflow_pb_s_kernel(
         psum = ctx.enter_context(tc.psum_pool(name="psum", bufs=BANKS))
         ctx.enter_context(tc.manual_schedule())
 
+        bias_row = keep.tile([P, D], BF16)
+        nc.sync.dma_start(out=bias_row[P - 1 : P, :], in_=gate_b.rearrange("(o n) -> o n", o=1))
+        nc.vector.memset(bias_row[0:96, :].bitcast(I32), 0)
+        nc.vector.memset(bias_row[96 : P - 1, :].bitcast(I32), 0)
         w_rows = keep.tile([P, PACK, D], BF16)
         nc.sync.dma_start(
             out=w_rows[:].rearrange("q (u e) n -> q u e n", u=HALVES),
             in_=gate_W.rearrange("(u q e) n -> q u e n", u=HALVES, e=2),
         )
-        bias_row = keep.tile([P, D], BF16)
-        nc.vector.memset(bias_row[:].bitcast(I32), 0)
-        nc.sync.dma_start(out=bias_row[0:1, :], in_=gate_b.rearrange("(o n) -> o n", o=1))
         x_rows = keep.tile([P, B * D], BF16)
         for b in range(B):
             nc.sync.dma_start(out=x_rows[:, b * D : (b + 1) * D], in_=token_embeddings[b])
@@ -72,13 +72,17 @@ def tile_splatinformationflow_pb_s_kernel(
         w_grouped = keep.tile([P, D, PACK], BF16, align_bytes=64)
         w_codes = keep.tile([P, D], U32, align_bytes=64)
         w_scales = keep.tile([P, D], U8, align_bytes=64)
-        w_cols = [slice(c * D // W_PARTS, (c + 1) * D // W_PARTS) for c in range(W_PARTS)]
-        for cols in w_cols:
-            nc.vector.tensor_copy(
+
+        def regroup(copy, cols):
+            copy(
                 out=w_grouped[:, cols, :].rearrange("p (c i) t -> p c t i", i=4),
                 in_=w_rows[:, :, cols].rearrange("p t (c i) -> p c t i", i=4),
             )
-        for cols in w_cols:
+
+        regroup(nc.scalar.copy, slice(3 * D // 4, D))
+        regroup(nc.vector.tensor_copy, slice(0, D // 2))
+        regroup(nc.vector.tensor_copy, slice(D // 2, 3 * D // 4))
+        for cols in (slice(0, D // 2), slice(D // 2, D)):
             nc.vector.quantize_mx(
                 out=w_codes[:, cols].bitcast(FP8X4),
                 scales=w_scales[:, cols],

@@ -39,13 +39,14 @@ def tile_splatinformationflow_pb_s_kernel(
         nc.sync.dma_start(out=bias_row[P - 1 : P, :], in_=gate_b.rearrange("(o n) -> o n", o=1))
         nc.vector.memset(bias_row[0:96, :].bitcast(I32), 0)
         nc.vector.memset(bias_row[96 : P - 1, :].bitcast(I32), 0)
+        x_rows = keep.tile([P, B * D], BF16)
+        nc.sync.dma_start(out=x_rows[:, 0:D], in_=token_embeddings[0])
         w_rows = keep.tile([P, PACK, D], BF16)
         nc.sync.dma_start(
             out=w_rows[:].rearrange("q (u e) n -> q u e n", u=HALVES),
             in_=gate_W.rearrange("(u q e) n -> q u e n", u=HALVES, e=2),
         )
-        x_rows = keep.tile([P, B * D], BF16)
-        for b in range(B):
+        for b in range(1, B):
             nc.sync.dma_start(out=x_rows[:, b * D : (b + 1) * D], in_=token_embeddings[b])
         infl_rows = keep.tile([P, ROWS, P], BF16)
         nc.sync.dma_start(

from contextlib import ExitStack

import concourse.mybir as mybir
from concourse.masks import make_identity

F32 = mybir.dt.float32
BF16 = mybir.dt.bfloat16
U32 = mybir.dt.uint32
U8 = mybir.dt.uint8
I32 = mybir.dt.int32
FP8X4 = mybir.dt.float8_e4m3fn_x4
ADD = mybir.AluOpType.add
MULT = mybir.AluOpType.mult
SIGMOID = mybir.ActivationFunctionType.Sigmoid

P = 128
B = 4
D = 512
PACK = 4
HALVES = 2
LAG = 2
BANKS = 8
ROWS = B

FLOPS = 2 * B * P * D * D + 2 * B * P * P * D


def tile_splatinformationflow_pb_s_kernel(
    tc, token_embeddings, splat_influences, decoded, gate_W, gate_b, out
):
    nc = tc.nc
    with ExitStack() as ctx:
        keep = ctx.enter_context(tc.tile_pool(name="keep", bufs=1))
        work = ctx.enter_context(tc.tile_pool(name="work", bufs=B))
        psum = ctx.enter_context(tc.psum_pool(name="psum", bufs=BANKS))
        ctx.enter_context(tc.manual_schedule())

        bias_row = keep.tile([P, D], BF16)
        nc.sync.dma_start(out=bias_row[P - 1 : P, :], in_=gate_b.rearrange("(o n) -> o n", o=1))
        nc.vector.memset(bias_row[0:96, :].bitcast(I32), 0)
        nc.vector.memset(bias_row[96 : P - 1, :].bitcast(I32), 0)
        x_rows = keep.tile([P, B * D], BF16)
        nc.sync.dma_start(out=x_rows[:, 0:D], in_=token_embeddings[0])
        w_rows = keep.tile([P, PACK, D], BF16)
        nc.sync.dma_start(
            out=w_rows[:].rearrange("q (u e) n -> q u e n", u=HALVES),
            in_=gate_W.rearrange("(u q e) n -> q u e n", u=HALVES, e=2),
        )
        for b in range(1, B):
            nc.sync.dma_start(out=x_rows[:, b * D : (b + 1) * D], in_=token_embeddings[b])
        infl_rows = keep.tile([P, ROWS, P], BF16)
        nc.sync.dma_start(
            out=infl_rows[:], in_=splat_influences.flatten_outer_dims().rearrange("(p r) k -> p r k", r=ROWS)
        )
        dec_rows = keep.tile([P, B, D], BF16)
        nc.sync.dma_start(out=dec_rows[:], in_=decoded.rearrange("b k d -> k b d"))

        warm = keep.tile([P, 1], F32)
        nc.vector.memset(warm[:], 0.0)
        nc.scalar.activation(out=warm[:], in_=warm[:], func=SIGMOID)
        ident_f32 = keep.tile([P, P], F32)
        make_identity(nc, ident_f32[:])
        ident_bf16 = keep.tile([P, P], BF16)
        make_identity(nc, ident_bf16[:])

        ones = keep.tile([P, P], BF16)
        nc.vector.memset(ones[:], 1.0)
        bias_ps = psum.tile([P, D], F32, tag="bank")
        nc.tensor.matmul(out=bias_ps[:], lhsT=ones[:], rhs=bias_row[:], start=True, stop=True)
        bias_all = keep.tile([P, D], F32)
        nc.scalar.copy(out=bias_all[:], in_=bias_ps[:])

        w_grouped = keep.tile([P, D, PACK], BF16, align_bytes=64)
        w_codes = keep.tile([P, D], U32, align_bytes=64)
        w_scales = keep.tile([P, D], U8, align_bytes=64)

        def regroup(copy, cols):
            copy(
                out=w_grouped[:, cols, :].rearrange("p (c i) t -> p c t i", i=4),
                in_=w_rows[:, :, cols].rearrange("p t (c i) -> p c t i", i=4),
            )

        regroup(nc.scalar.copy, slice(3 * D // 4, D))
        regroup(nc.vector.tensor_copy, slice(0, D // 2))
        regroup(nc.vector.tensor_copy, slice(D // 2, 3 * D // 4))
        for cols in (slice(0, D // 2), slice(D // 2, D)):
            nc.vector.quantize_mx(
                out=w_codes[:, cols].bitcast(FP8X4),
                scales=w_scales[:, cols],
                in_=w_grouped[:, cols, :].rearrange("p n t -> p (n t)"),
            )

        x_words = x_rows[:].bitcast(F32)
        x_grouped = keep.tile([P, B * P * PACK], BF16, align_bytes=64)
        x_grouped_words = x_grouped[:].bitcast(F32)
        x_codes = keep.tile([P, B * P], U32, align_bytes=64)
        x_scales = keep.tile([P, B * P], U8, align_bytes=64)
        for b in range(B):
            xt_ps = psum.tile([P, HALVES, P], F32, tag="bank")
            for u in range(HALVES):
                first = (b * HALVES + u) * P
                nc.tensor.transpose(xt_ps[:, u, :], x_words[:, first : first + P], ident_f32[:])
            nc.scalar.copy(
                out=x_grouped_words[:, b * P * HALVES : (b + 1) * P * HALVES].rearrange("p (s u) -> p s u", u=HALVES),
                in_=xt_ps[:].rearrange("p u s -> p s u"),
            )
            nc.vector.quantize_mx(
                out=x_codes[:, b * P : (b + 1) * P].bitcast(FP8X4),
                scales=x_scales[:, b * P : (b + 1) * P],
                in_=x_grouped[:, b * P * PACK : (b + 1) * P * PACK],
            )

        inflT_ps = psum.tile([P, ROWS, P], BF16, tag="bank")
        for r in range(ROWS):
            nc.tensor.transpose(inflT_ps[:, r, :], infl_rows[:, r, :], ident_bf16[:])
        inflT = keep.tile([P, B * P], BF16)
        nc.scalar.copy(out=inflT[:].rearrange("k (p r) -> k p r", r=ROWS), in_=inflT_ps[:].rearrange("k r p -> k p r"))

        gates = []

        def gate_of(b):
            gate_ps = psum.tile([P, D], F32, tag="bank")
            nc.tensor.matmul_mx(
                out=gate_ps[:],
                lhsT=x_codes[:, b * P : (b + 1) * P].bitcast(FP8X4),
                lhsT_scale=x_scales[:, b * P : (b + 1) * P],
                rhs=w_codes[:].bitcast(FP8X4),
                rhs_scale=w_scales[:],
                start=True,
                stop=True,
            )
            logits = work.tile([P, D], F32)
            nc.vector.tensor_tensor(out=logits[:], in0=gate_ps[:], in1=bias_all[:], op=ADD)
            gate = work.tile([P, D], F32)
            nc.scalar.activation(out=gate[:], in_=logits[:], func=SIGMOID)
            gates.append(gate)

        def gated_flow_of(b):
            flow_ps = psum.tile([P, D], F32, tag="bank")
            nc.tensor.matmul(out=flow_ps[:], lhsT=inflT[:, b * P : (b + 1) * P], rhs=dec_rows[:, b, :], start=True, stop=True)
            result = work.tile([P, D], F32)
            nc.vector.tensor_tensor(out=result[:], in0=flow_ps[:], in1=gates[b][:], op=MULT)
            nc.sync.dma_start(out=out[b], in_=result[:])

        for b in range(B + LAG):
            if b < B:
                gate_of(b)
            if b >= LAG:
                gated_flow_of(b - LAG)
